import numpy as np
import ml_dtypes


def mxq(x, axis, fmt="e4m3"):
    dtype, down = {"e4m3": (ml_dtypes.float8_e4m3fn, 7), "e5m2": (ml_dtypes.float8_e5m2, 14)}[fmt]
    v = np.moveaxis(np.asarray(x, np.float32).astype(ml_dtypes.bfloat16).astype(np.float64), axis, -1)
    blocks = v.reshape(v.shape[:-1] + (-1, 32))
    amax = np.abs(blocks).max(-1, keepdims=True)
    byte = np.maximum(np.where(amax > 0, np.frexp(amax)[1] - 1 + 127, 0) - down, 1)
    scale = np.exp2(byte - 127.0)
    codes = (blocks / scale).astype(np.float32).astype(dtype).astype(np.float64)
    return np.moveaxis((codes * scale).reshape(v.shape), -1, axis)


WIDE = False


def mx_kscale(k):
    if not WIDE:
        return np.ones(k)
    levels = np.array([10, -10, 5, -5, 0])
    if k % 512:
        return np.exp2(np.random.permutation(np.resize(levels, k // 32))).repeat(32)
    a = np.empty((k // 512, 16))
    for p in range(k // 512):
        a[p, :8] = np.random.permutation(np.resize(levels, 8))
        for g in range(8):
            far = levels[np.abs(levels - a[p, g]) >= 10]
            a[p, g + 8] = far[np.random.randint(len(far))]
    return np.exp2(a.ravel()).repeat(32)


BF16 = ml_dtypes.bfloat16


def bf(x):
    return np.asarray(x, np.float32).astype(BF16)


def f64(x):
    return np.asarray(x).astype(np.float64)


B, H, W, C, NH, WS, SHIFT, F = 4, 16, 16, 1024, 32, 8, 3, 4096
S = WS * WS
HD = C // NH
EPS = 1e-5


def layer_norm(x, w, b):
    m = x.mean(-1, keepdims=True)
    v = ((x - m) ** 2).mean(-1, keepdims=True)
    return (x - m) / np.sqrt(v + EPS) * w + b


def to_heads(t):
    return t.reshape(-1, S, NH, HD).transpose(0, 2, 1, 3)


def setup_inputs():
    s = mx_kscale(C)
    return {"x": bf(np.random.standard_normal((B, H * W, C))),
            "norm1_w": bf((1.0 + 0.1 * np.random.standard_normal(C)) * s),
            "norm1_b": bf(0.1 * np.random.standard_normal(C) * s),
            "qkv_w": bf(np.random.standard_normal((3 * C, C)) / np.sqrt(C) / s[None, :]),
            "qkv_b": bf(0.1 * np.random.standard_normal(3 * C))}


def reference(x, norm1_w, norm1_b, qkv_w, qkv_b):
    h = layer_norm(f64(x), f64(norm1_w), f64(norm1_b)).reshape(B, H, W, C)
    h = np.roll(h, (-SHIFT, -SHIFT), axis=(1, 2))
    win = h.reshape(B, H // WS, WS, W // WS, WS, C)
    win = win.transpose(0, 1, 3, 2, 4, 5).reshape(-1, S, C)
    win = win
    qkv = (mxq(win, 2, "e4m3") @ mxq(f64(qkv_w), 1, "e4m3").T) + f64(qkv_b)
    q, k, v = np.split(qkv, 3, axis=-1)
    return to_heads(q), to_heads(k), to_heads(v)

@@ -1,0 +1,287 @@
+from contextlib import ExitStack
+
+import concourse.mybir as mybir
+from concourse.masks import make_identity
+
+F32 = mybir.dt.float32
+BF16 = mybir.dt.bfloat16
+U32 = mybir.dt.uint32
+U8 = mybir.dt.uint8
+FP8X4 = mybir.dt.float8_e4m3fn_x4
+ALU = mybir.AluOpType
+ACT = mybir.ActivationFunctionType
+
+P = 128
+C = 1024
+EPS = 1e-5
+IMAGES, GRID, WS, SHIFT = 4, 16, 8, 3
+HD = 32
+PACK = 4
+PASSES = C // (P * PACK)
+PLANES = C // P
+PAIRS = PACK // 2
+PAIR = 2
+N_PAIRS = WS // PAIR
+N_COLS = 256
+N_SLABS = 3 * C // N_COLS
+ROW_TILES = N_COLS // P
+HEADS = N_COLS // HD
+BANKS = 8
+FLIP_LAG = 3
+SCALE_LAG = 4
+
+FLOPS = 2 * IMAGES * GRID * GRID * C * 3 * C
+
+
+def tile_swintransformerblock_pa_kernel(
+    tc, x, norm1_w, norm1_b, qkv_w, qkv_b, out_0, out_1, out_2
+):
+    nc = tc.nc
+    outs = (out_0, out_1, out_2)
+
+    with ExitStack() as ctx:
+        ctx.enter_context(tc.manual_schedule())
+        const = ctx.enter_context(tc.tile_pool(name="const", bufs=1))
+        small = ctx.enter_context(tc.tile_pool(name="small", bufs=4))
+        centred_pool = ctx.enter_context(tc.tile_pool(name="centred", bufs=3))
+        work = ctx.enter_context(tc.tile_pool(name="work", bufs=2))
+        slab_pool = ctx.enter_context(tc.tile_pool(name="slab", bufs=4))
+        stage_pool = ctx.enter_context(tc.tile_pool(name="stage", bufs=4))
+        psum = ctx.enter_context(tc.psum_pool(name="psum", bufs=BANKS))
+
+        x_raw = const.tile([P, WS, C], BF16)
+        x_rows = x.rearrange("b (q e) k -> (b q) e k", e=WS)
+        w_raw = [const.tile([P, ROW_TILES, C], BF16, name="w_raw%d" % s) for s in range(N_SLABS)]
+        bias_row = const.tile([P, 3 * C], BF16)
+        nc.gpsimd.memset(bias_row[:].bitcast(F32), 0.0)
+        bias_all = const.tile([P, 3 * C], F32)
+
+        def tile_of(c):
+            return (c + SHIFT) % WS
+
+        def load_tokens(first, last):
+            nc.sync.dma_start(out=x_raw[:, first:last, :], in_=x_rows[:, first:last, :])
+
+        def load_weights(s):
+            rows = qkv_w[N_COLS * s : N_COLS * (s + 1), :]
+            nc.sync.dma_start(out=w_raw[s][:], in_=rows.rearrange("(j p) k -> p j k", p=P))
+
+        load_tokens(SHIFT, SHIFT + 1)
+        load_tokens(SHIFT + 1, SHIFT + 3)
+        load_weights(0)
+        load_tokens(SHIFT + 3, WS)
+        load_weights(1)
+        load_tokens(0, SHIFT)
+        for s in range(2, N_SLABS):
+            load_weights(s)
+
+        gain_bf = const.tile([P, PASSES, PACK], BF16)
+        beta_bf = const.tile([P, PASSES, PACK], BF16)
+        with nc.allow_non_contiguous_dma(reason="two small vectors, four channels a piece"):
+            nc.scalar.dma_start(out=gain_bf[:], in_=norm1_w.rearrange("(g p t) -> p g t", p=P, t=PACK))
+            nc.scalar.dma_start(out=beta_bf[:], in_=norm1_b.rearrange("(g p t) -> p g t", p=P, t=PACK))
+        nc.scalar.dma_start(out=bias_row[0:1, :], in_=qkv_b.rearrange("(o n) -> o n", o=1))
+        gain = const.tile([P, PLANES], F32)
+        beta = const.tile([P, PLANES], F32)
+
+        warm = const.tile([P, 2], F32)
+        nc.vector.memset(warm[:, 0:1], 1.0)
+        nc.scalar.activation(out=warm[:, 1:2], in_=warm[:, 0:1], func=ACT.Sqrt)
+        ones = const.tile([P, P], BF16)
+        nc.vector.memset(ones[:], 1.0)
+
+        ident = const.tile([P, P], F32)
+        make_identity(nc, ident[:])
+        by_grid = ident[:].rearrange("p (b i h) -> p b h i", b=IMAGES, h=2)
+        roll_same = const.tile([P, P], F32)
+        same = roll_same[:].rearrange("p (b wi wj r) -> p b wi wj r", b=IMAGES, wi=2, wj=2)
+        wrap = GRID - WS - SHIFT
+        nc.vector.tensor_copy(out=same[:, :, 0, :, :], in_=by_grid[:, :, :, SHIFT : SHIFT + WS])
+        nc.vector.tensor_copy(out=same[:, :, 1, :, 0:wrap], in_=by_grid[:, :, :, SHIFT + WS : GRID])
+        nc.vector.tensor_copy(out=same[:, :, 1, :, wrap:WS], in_=by_grid[:, :, :, 0:SHIFT])
+        roll_swap = const.tile([P, P], F32)
+        swap = roll_swap[:].rearrange("p (b wi wj r) -> p b wi wj r", b=IMAGES, wi=2, wj=2)
+        nc.vector.tensor_copy(out=swap[:, :, :, 0, :], in_=same[:, :, :, 1, :])
+        nc.vector.tensor_copy(out=swap[:, :, :, 1, :], in_=same[:, :, :, 0, :])
+
+        x_codes = const.tile([P, N_PAIRS, PASSES, PAIR * P], U32, align_bytes=64)
+        x_scales = const.tile([P, N_PAIRS, PASSES, PAIR * P], U8, align_bytes=64)
+        w_codes = [
+            const.tile([P, PASSES, N_COLS], U32, name="w_codes%d" % s, align_bytes=64)
+            for s in range(N_SLABS)
+        ]
+        w_scales = [
+            const.tile([P, PASSES, N_COLS], U8, name="w_scales%d" % s, align_bytes=64)
+            for s in range(N_SLABS)
+        ]
+        mean_var = const.tile([P, WS, 2], F32)
+        std = const.tile([P, WS], F32)
+        neg_mean = const.tile([P, WS], F32)
+        rstd = const.tile([P, WS], F32)
+        planes = [const.tile([P, PLANES, PAIR * P], BF16, name="planes%d" % q) for q in range(N_PAIRS)]
+        centred = {}
+        flipped = {}
+        grouped = {}
+        w_grouped = {}
+
+        def statistics(c):
+            stats = small.tile([P, 2, 6], F32)
+            for half in range(2):
+                nc.vector.bn_stats(
+                    out=stats[:, half, :],
+                    in_=x_raw[:, tile_of(c), (C // 2) * half : (C // 2) * (half + 1)],
+                )
+            nc.vector.bn_aggr(out=mean_var[:, c, :], in_=stats[:].rearrange("p h s -> p (h s)"))
+            nc.scalar.activation(
+                out=std[:, c : c + 1], in_=mean_var[:, c, 1:2], func=ACT.Sqrt, bias=EPS, scale=1.0
+            )
+            nc.scalar.activation(
+                out=neg_mean[:, c : c + 1], in_=mean_var[:, c, 0:1], func=ACT.Identity, scale=-1.0
+            )
+
+        def centre(c):
+            nc.vector.reciprocal(out=rstd[:, c : c + 1], in_=std[:, c : c + 1])
+            q, i = divmod(c, PAIR)
+            if i == 0:
+                centred[q] = centred_pool.tile([P, PAIR, C], F32, name="centred")
+            nc.gpsimd.tensor_scalar(
+                out=centred[q][:, i, :].rearrange("p (g t k) -> p g t k", g=PASSES, t=PACK),
+                in0=x_raw[:, tile_of(c), :].rearrange("p (g k t) -> p g t k", g=PASSES, t=PACK),
+                scalar1=neg_mean[:, c : c + 1],
+                scalar2=rstd[:, c : c + 1],
+                op0=ALU.add,
+                op1=ALU.mult,
+            )
+
+        def flip_tokens(q, g):
+            flipped[q, g] = []
+            for u in range(2):
+                bank = psum.tile([P, 2, PAIR, P], F32, tag="bank", name="flipped")
+                for e in range(2):
+                    plane = PACK * g + 2 * u + e
+                    for i in range(PAIR):
+                        nc.tensor.transpose(
+                            out=bank[:, e, i, :],
+                            in_=centred[q][:, i, P * plane : P * (plane + 1)],
+                            identity=(roll_same if PAIR * q + i < WS - SHIFT else roll_swap)[:],
+                        )
+                flipped[q, g].append(bank)
+
+        def scale_tokens(q, g):
+            for u in range(2):
+                for e in range(2):
+                    plane = PACK * g + 2 * u + e
+                    nc.scalar.activation(
+                        out=planes[q][:, plane, :],
+                        in_=flipped[q, g][u][:, e, :, :].rearrange("p i m -> p (i m)"),
+                        func=ACT.Identity,
+                        scale=gain[:, plane : plane + 1],
+                        bias=beta[:, plane : plane + 1],
+                    )
+
+        def regroup_tokens(q, g):
+            if g == 0:
+                grouped[q] = work.tile([P, PASSES, PAIR * P, PACK], BF16, name="grouped", align_bytes=64)
+            nc.vector.tensor_copy(
+                out=grouped[q][:, g, :, :].rearrange("p (m i) t -> p m t i", i=4),
+                in_=planes[q][:, PACK * g : PACK * (g + 1), :].rearrange("p t (m i) -> p m t i", i=4),
+            )
+
+        def quantise_tokens(q, g):
+            nc.vector.quantize_mx(
+                out=x_codes[:, q, g, :].bitcast(FP8X4),
+                scales=x_scales[:, q, g, :],
+                in_=grouped[q][:, g, :, :].rearrange("p m t -> p (m t)"),
+            )
+
+        def flip_weights(s):
+            words = w_raw[s][:].bitcast(F32)
+            w_grouped[s] = slab_pool.tile([P, PASSES, N_COLS, PACK], BF16, name="w_grouped", align_bytes=64)
+            grouped_words = w_grouped[s][:].bitcast(F32)
+            for g in range(PASSES):
+                bank = psum.tile([P, 2, N_COLS], F32, tag="bank", name="w_flipped")
+                for u in range(PAIRS):
+                    for j in range(ROW_TILES):
+                        nc.tensor.transpose(
+                            out=bank[:, u, P * j : P * (j + 1)],
+                            in_=words[:, j, PAIRS * P * g + u : PAIRS * P * (g + 1) : PAIRS],
+                            identity=ident[:],
+                        )
+                nc.scalar.copy(out=grouped_words[:, g, :, :], in_=bank[:].rearrange("p u c -> p c u"))
+            cols = slice(N_COLS * s, N_COLS * (s + 1))
+            spread = psum.tile([P, N_COLS], F32, tag="bank")
+            nc.tensor.matmul(out=spread[:], lhsT=ones[:], rhs=bias_row[:, cols], start=True, stop=True)
+            nc.scalar.copy(out=bias_all[:, cols], in_=spread[:])
+
+        def quantise_weights(s):
+            nc.vector.quantize_mx(
+                out=w_codes[s][:].rearrange("p g c -> p (g c)").bitcast(FP8X4),
+                scales=w_scales[s][:].rearrange("p g c -> p (g c)"),
+                in_=w_grouped[s][:].rearrange("p g c t -> p (g c t)"),
+            )
+
+        def project(s):
+            stage = stage_pool.tile([P, HEADS, WS, HD], F32)
+            bias = (
+                bias_all[:, N_COLS * s : N_COLS * (s + 1)]
+                .rearrange("p (a d) -> p a d", d=HD)
+                .unsqueeze(2)
+                .to_broadcast([P, HEADS, PAIR, HD])
+            )
+            for q in range(N_PAIRS):
+                acc = psum.tile([P, PAIR, N_COLS], F32, tag="bank")
+                for i in range(PAIR):
+                    tokens = slice(P * i, P * (i + 1))
+                    for g in range(PASSES):
+                        nc.tensor.matmul_mx(
+                            out=acc[:, i, :],
+                            lhsT=x_codes[:, q, g, tokens].bitcast(FP8X4),
+                            lhsT_scale=x_scales[:, q, g, tokens],
+                            rhs=w_codes[s][:, g, :].bitcast(FP8X4),
+                            rhs_scale=w_scales[s][:, g, :],
+                            start=(g == 0),
+                            stop=(g == PASSES - 1),
+                        )
+                nc.vector.tensor_tensor(
+                    out=stage[:, :, PAIR * q : PAIR * (q + 1), :],
+                    in0=acc[:].rearrange("p i (a d) -> p a i d", d=HD),
+                    in1=bias,
+                    op=ALU.add,
+                )
+            slabs_per_output = C // N_COLS
+            rows_of = outs[s // slabs_per_output].rearrange("w a (r c) d -> a w r (c d)", c=WS)
+            first_head = HEADS * (s % slabs_per_output)
+            for a in range(HEADS):
+                nc.sync.dma_start(
+                    out=rows_of[first_head + a], in_=stage[:, a, :, :].rearrange("p c d -> p (c d)")
+                )
+
+        for step in range(WS + SCALE_LAG):
+            if step < WS:
+                statistics(step)
+            if 1 <= step <= WS:
+                centre(step - 1)
+            if 1 <= step < FLIP_LAG:
+                flip_weights(step - 1)
+            if step == FLIP_LAG:
+                nc.vector.tensor_copy(out=gain[:], in_=gain_bf[:].rearrange("p g t -> p (g t)"))
+                nc.vector.tensor_copy(out=beta[:], in_=beta_bf[:].rearrange("p g t -> p (g t)"))
+            if 0 <= step - FLIP_LAG < WS:
+                flip_tokens(*divmod(step - FLIP_LAG, PASSES))
+            if 0 <= step - SCALE_LAG < WS:
+                scale_tokens(*divmod(step - SCALE_LAG, PASSES))
+        quantise_weights(0)
+        for unit in range(WS + 1):
+            if unit < WS:
+                regroup_tokens(*divmod(unit, PASSES))
+            if unit > 0:
+                quantise_tokens(*divmod(unit - 1, PASSES))
+
+        for s in range(0, N_SLABS, 2):
+            project(s)
+            quantise_weights(s + 1)
+            if s + 2 < N_SLABS:
+                flip_weights(s + 2)
+                flip_weights(s + 3)
+                quantise_weights(s + 2)
+            project(s + 1)

@@ -46,6 +46,7 @@ def tile_swintransformerblock_pa_kernel(
         centred_pool = ctx.enter_context(tc.tile_pool(name="centred", bufs=3))
         work = ctx.enter_context(tc.tile_pool(name="work", bufs=2))
         slab_pool = ctx.enter_context(tc.tile_pool(name="slab", bufs=4))
+        sorted_pool = ctx.enter_context(tc.tile_pool(name="sorted", bufs=4))
         stage_pool = ctx.enter_context(tc.tile_pool(name="stage", bufs=4))
         psum = ctx.enter_context(tc.psum_pool(name="psum", bufs=BANKS))
 
@@ -53,8 +54,9 @@ def tile_swintransformerblock_pa_kernel(
         x_rows = x.rearrange("b (q e) k -> (b q) e k", e=WS)
         w_raw = [const.tile([P, ROW_TILES, C], BF16, name="w_raw%d" % s) for s in range(N_SLABS)]
         bias_row = const.tile([P, 3 * C], BF16)
-        nc.gpsimd.memset(bias_row[:].bitcast(F32), 0.0)
-        bias_all = const.tile([P, 3 * C], F32)
+        nc.vector.memset(bias_row[:].bitcast(F32), 0.0)
+        nc.scalar.dma_start(out=bias_row[0:1, :], in_=qkv_b.rearrange("(o n) -> o n", o=1))
+        bias_all = const.tile([P, 3 * C], BF16)
 
         def tile_of(c):
             return (c + SHIFT) % WS
@@ -64,7 +66,7 @@ def tile_swintransformerblock_pa_kernel(
 
         def load_weights(s):
             rows = qkv_w[N_COLS * s : N_COLS * (s + 1), :]
-            nc.sync.dma_start(out=w_raw[s][:], in_=rows.rearrange("(j p) k -> p j k", p=P))
+            nc.sync.dma_start(out=w_raw[s][:], in_=rows.rearrange("(p j) k -> p j k", p=P))
 
         load_tokens(SHIFT, SHIFT + 1)
         load_tokens(SHIFT + 1, SHIFT + 3)
@@ -80,7 +82,6 @@ def tile_swintransformerblock_pa_kernel(
         with nc.allow_non_contiguous_dma(reason="two small vectors, four channels a piece"):
             nc.scalar.dma_start(out=gain_bf[:], in_=norm1_w.rearrange("(g p t) -> p g t", p=P, t=PACK))
             nc.scalar.dma_start(out=beta_bf[:], in_=norm1_b.rearrange("(g p t) -> p g t", p=P, t=PACK))
-        nc.scalar.dma_start(out=bias_row[0:1, :], in_=qkv_b.rearrange("(o n) -> o n", o=1))
         gain = const.tile([P, PLANES], F32)
         beta = const.tile([P, PLANES], F32)
 
@@ -122,6 +123,7 @@ def tile_swintransformerblock_pa_kernel(
         centred = {}
         flipped = {}
         grouped = {}
+        w_sorted = {}
         w_grouped = {}
 
         def statistics(c):
@@ -194,24 +196,46 @@ def tile_swintransformerblock_pa_kernel(
                 in_=grouped[q][:, g, :, :].rearrange("p m t -> p (m t)"),
             )
 
+        def spread_bias(part):
+            half = C // 2
+            spread = psum.tile([P, C], BF16, tag="bank")
+            for h in range(2):
+                nc.tensor.matmul(
+                    out=spread[:, half * h : half * (h + 1)],
+                    lhsT=ones[:],
+                    rhs=bias_row[:, C * part + half * h : C * part + half * (h + 1)],
+                    start=True,
+                    stop=True,
+                )
+            nc.scalar.copy(out=bias_all[:, C * part : C * (part + 1)], in_=spread[:])
+
+        def sort_weights(s):
+            w_sorted[s] = sorted_pool.tile([P, ROW_TILES, PASSES, PAIRS, P], F32, name="w_sorted")
+            nc.scalar.copy(
+                out=w_sorted[s][:].rearrange("p j g u k -> p (j g) u k"),
+                in_=w_raw[s][:].bitcast(F32).rearrange("p j (g k u) -> p (j g) u k", g=PASSES, u=PAIRS),
+            )
+
         def flip_weights(s):
-            words = w_raw[s][:].bitcast(F32)
+            if s in w_sorted:
+                words = w_sorted[s][:]
+            else:
+                words = w_raw[s][:].bitcast(F32).rearrange("p j (g k u) -> p j g u k", g=PASSES, u=PAIRS)
             w_grouped[s] = slab_pool.tile([P, PASSES, N_COLS, PACK], BF16, name="w_grouped", align_bytes=64)
             grouped_words = w_grouped[s][:].bitcast(F32)
             for g in range(PASSES):
-                bank = psum.tile([P, 2, N_COLS], F32, tag="bank", name="w_flipped")
+                bank = psum.tile([P, PAIRS, ROW_TILES, P], F32, tag="bank", name="w_flipped")
                 for u in range(PAIRS):
                     for j in range(ROW_TILES):
                         nc.tensor.transpose(
-                            out=bank[:, u, P * j : P * (j + 1)],
-                            in_=words[:, j, PAIRS * P * g + u : PAIRS * P * (g + 1) : PAIRS],
+                            out=bank[:, u, j, :],
+                            in_=words[:, j, g, u, :],
                             identity=ident[:],
                         )
-                nc.scalar.copy(out=grouped_words[:, g, :, :], in_=bank[:].rearrange("p u c -> p c u"))
-            cols = slice(N_COLS * s, N_COLS * (s + 1))
-            spread = psum.tile([P, N_COLS], F32, tag="bank")
-            nc.tensor.matmul(out=spread[:], lhsT=ones[:], rhs=bias_row[:, cols], start=True, stop=True)
-            nc.scalar.copy(out=bias_all[:, cols], in_=spread[:])
+                nc.scalar.copy(
+                    out=grouped_words[:, g, :, :].rearrange("p (m j) u -> p m j u", j=ROW_TILES),
+                    in_=bank[:].rearrange("p u j m -> p m j u"),
+                )
 
         def quantise_weights(s):
             nc.vector.quantize_mx(
@@ -264,12 +288,15 @@ def tile_swintransformerblock_pa_kernel(
             if 1 <= step < FLIP_LAG:
                 flip_weights(step - 1)
             if step == FLIP_LAG:
+                spread_bias(0)
                 nc.vector.tensor_copy(out=gain[:], in_=gain_bf[:].rearrange("p g t -> p (g t)"))
                 nc.vector.tensor_copy(out=beta[:], in_=beta_bf[:].rearrange("p g t -> p (g t)"))
             if 0 <= step - FLIP_LAG < WS:
                 flip_tokens(*divmod(step - FLIP_LAG, PASSES))
             if 0 <= step - SCALE_LAG < WS:
                 scale_tokens(*divmod(step - SCALE_LAG, PASSES))
+        spread_bias(1)
+        spread_bias(2)
         quantise_weights(0)
         for unit in range(WS + 1):
             if unit < WS:
@@ -277,6 +304,8 @@ def tile_swintransformerblock_pa_kernel(
             if unit > 0:
                 quantise_tokens(*divmod(unit - 1, PASSES))
 
+        sort_weights(2)
+        sort_weights(3)
         for s in range(0, N_SLABS, 2):
             project(s)
             quantise_weights(s + 1)
@@ -284,4 +313,7 @@ def tile_swintransformerblock_pa_kernel(
                 flip_weights(s + 2)
                 flip_weights(s + 3)
                 quantise_weights(s + 2)
+            if s + 4 < N_SLABS:
+                sort_weights(s + 4)
+                sort_weights(s + 5)
             project(s + 1)

@@ -27,8 +27,7 @@ N_SLABS = 3 * C // N_COLS
 ROW_TILES = N_COLS // P
 HEADS = N_COLS // HD
 BANKS = 8
-FLIP_LAG = 3
-SCALE_LAG = 4
+BANK_F32 = 512
 
 FLOPS = 2 * IMAGES * GRID * GRID * C * 3 * C
 
@@ -44,9 +43,9 @@ def tile_swintransformerblock_pa_kernel(
         const = ctx.enter_context(tc.tile_pool(name="const", bufs=1))
         small = ctx.enter_context(tc.tile_pool(name="small", bufs=4))
         centred_pool = ctx.enter_context(tc.tile_pool(name="centred", bufs=3))
-        work = ctx.enter_context(tc.tile_pool(name="work", bufs=2))
+        work = ctx.enter_context(tc.tile_pool(name="work", bufs=4))
         slab_pool = ctx.enter_context(tc.tile_pool(name="slab", bufs=4))
-        sorted_pool = ctx.enter_context(tc.tile_pool(name="sorted", bufs=4))
+        sorted_pool = ctx.enter_context(tc.tile_pool(name="sorted", bufs=3))
         stage_pool = ctx.enter_context(tc.tile_pool(name="stage", bufs=4))
         psum = ctx.enter_context(tc.psum_pool(name="psum", bufs=BANKS))
 
@@ -54,8 +53,10 @@ def tile_swintransformerblock_pa_kernel(
         x_rows = x.rearrange("b (q e) k -> (b q) e k", e=WS)
         w_raw = [const.tile([P, ROW_TILES, C], BF16, name="w_raw%d" % s) for s in range(N_SLABS)]
         bias_row = const.tile([P, 3 * C], BF16)
+        warm = const.tile([P, 2], F32)
+        nc.vector.memset(warm[:, 0:1], 1.0)
+        nc.scalar.activation(out=warm[:, 1:2], in_=warm[:, 0:1], func=ACT.Sqrt)
         nc.vector.memset(bias_row[:].bitcast(F32), 0.0)
-        nc.scalar.dma_start(out=bias_row[0:1, :], in_=qkv_b.rearrange("(o n) -> o n", o=1))
         bias_all = const.tile([P, 3 * C], BF16)
 
         def tile_of(c):
@@ -68,13 +69,15 @@ def tile_swintransformerblock_pa_kernel(
             rows = qkv_w[N_COLS * s : N_COLS * (s + 1), :]
             nc.sync.dma_start(out=w_raw[s][:], in_=rows.rearrange("(p j) k -> p j k", p=P))
 
-        load_tokens(SHIFT, SHIFT + 1)
-        load_tokens(SHIFT + 1, SHIFT + 3)
+        for half in range(2):
+            channels = slice((C // 2) * half, (C // 2) * (half + 1))
+            nc.sync.dma_start(out=x_raw[:, SHIFT, channels], in_=x_rows[:, SHIFT, channels])
+        load_tokens(SHIFT + 1, SHIFT + 2)
+        load_tokens(SHIFT + 2, SHIFT + 4)
         load_weights(0)
-        load_tokens(SHIFT + 3, WS)
-        load_weights(1)
+        load_tokens(SHIFT + 4, WS)
         load_tokens(0, SHIFT)
-        for s in range(2, N_SLABS):
+        for s in range(1, N_SLABS):
             load_weights(s)
 
         gain_bf = const.tile([P, PASSES, PACK], BF16)
@@ -82,12 +85,10 @@ def tile_swintransformerblock_pa_kernel(
         with nc.allow_non_contiguous_dma(reason="two small vectors, four channels a piece"):
             nc.scalar.dma_start(out=gain_bf[:], in_=norm1_w.rearrange("(g p t) -> p g t", p=P, t=PACK))
             nc.scalar.dma_start(out=beta_bf[:], in_=norm1_b.rearrange("(g p t) -> p g t", p=P, t=PACK))
+        nc.scalar.dma_start(out=bias_row[0:1, :], in_=qkv_b.rearrange("(o n) -> o n", o=1))
         gain = const.tile([P, PLANES], F32)
         beta = const.tile([P, PLANES], F32)
 
-        warm = const.tile([P, 2], F32)
-        nc.vector.memset(warm[:, 0:1], 1.0)
-        nc.scalar.activation(out=warm[:, 1:2], in_=warm[:, 0:1], func=ACT.Sqrt)
         ones = const.tile([P, P], BF16)
         nc.vector.memset(ones[:], 1.0)
 
@@ -117,23 +118,29 @@ def tile_swintransformerblock_pa_kernel(
         ]
         mean_var = const.tile([P, WS, 2], F32)
         std = const.tile([P, WS], F32)
+        sums = const.tile([P, WS, 2], F32)
+        ignored = const.tile([P, C], BF16)
         neg_mean = const.tile([P, WS], F32)
         rstd = const.tile([P, WS], F32)
         planes = [const.tile([P, PLANES, PAIR * P], BF16, name="planes%d" % q) for q in range(N_PAIRS)]
+        stats = {}
         centred = {}
         flipped = {}
         grouped = {}
         w_sorted = {}
+        w_flipped = {}
         w_grouped = {}
 
+        def sums_of(c, half):
+            if half == 0:
+                stats[c] = small.tile([P, 2, 6], F32, name="stats")
+            nc.vector.bn_stats(
+                out=stats[c][:, half, :],
+                in_=x_raw[:, tile_of(c), (C // 2) * half : (C // 2) * (half + 1)],
+            )
+
         def statistics(c):
-            stats = small.tile([P, 2, 6], F32)
-            for half in range(2):
-                nc.vector.bn_stats(
-                    out=stats[:, half, :],
-                    in_=x_raw[:, tile_of(c), (C // 2) * half : (C // 2) * (half + 1)],
-                )
-            nc.vector.bn_aggr(out=mean_var[:, c, :], in_=stats[:].rearrange("p h s -> p (h s)"))
+            nc.vector.bn_aggr(out=mean_var[:, c, :], in_=stats[c][:].rearrange("p h s -> p (h s)"))
             nc.scalar.activation(
                 out=std[:, c : c + 1], in_=mean_var[:, c, 1:2], func=ACT.Sqrt, bias=EPS, scale=1.0
             )
@@ -141,12 +148,34 @@ def tile_swintransformerblock_pa_kernel(
                 out=neg_mean[:, c : c + 1], in_=mean_var[:, c, 0:1], func=ACT.Identity, scale=-1.0
             )
 
-        def centre(c):
+        def scalar_sum(c):
+            nc.scalar.activation(
+                out=ignored[:], in_=x_raw[:, tile_of(c), :], func=ACT.Identity, accum_out=sums[:, c, 0:1]
+            )
+            nc.scalar.activation(
+                out=neg_mean[:, c : c + 1], in_=sums[:, c, 0:1], func=ACT.Identity, scale=-1.0 / C
+            )
+
+        def scalar_variance(c):
+            nc.scalar.activation(
+                out=ignored[:],
+                in_=x_raw[:, tile_of(c), :],
+                func=ACT.Square,
+                bias=neg_mean[:, c : c + 1],
+                accum_out=sums[:, c, 1:2],
+            )
+            nc.scalar.activation(
+                out=std[:, c : c + 1], in_=sums[:, c, 1:2], func=ACT.Sqrt, bias=EPS, scale=1.0 / C
+            )
+
+        def invert(c):
             nc.vector.reciprocal(out=rstd[:, c : c + 1], in_=std[:, c : c + 1])
+
+        def centre(engine, c):
             q, i = divmod(c, PAIR)
             if i == 0:
                 centred[q] = centred_pool.tile([P, PAIR, C], F32, name="centred")
-            nc.gpsimd.tensor_scalar(
+            engine.tensor_scalar(
                 out=centred[q][:, i, :].rearrange("p (g t k) -> p g t k", g=PASSES, t=PACK),
                 in0=x_raw[:, tile_of(c), :].rearrange("p (g k t) -> p g t k", g=PASSES, t=PACK),
                 scalar1=neg_mean[:, c : c + 1],
@@ -181,10 +210,10 @@ def tile_swintransformerblock_pa_kernel(
                         bias=beta[:, plane : plane + 1],
                     )
 
-        def regroup_tokens(q, g):
-            if g == 0:
+        def regroup_tokens(q, g, copy=nc.vector.tensor_copy):
+            if q not in grouped:
                 grouped[q] = work.tile([P, PASSES, PAIR * P, PACK], BF16, name="grouped", align_bytes=64)
-            nc.vector.tensor_copy(
+            copy(
                 out=grouped[q][:, g, :, :].rearrange("p (m i) t -> p m t i", i=4),
                 in_=planes[q][:, PACK * g : PACK * (g + 1), :].rearrange("p t (m i) -> p m t i", i=4),
             )
@@ -221,20 +250,21 @@ def tile_swintransformerblock_pa_kernel(
                 words = w_sorted[s][:]
             else:
                 words = w_raw[s][:].bitcast(F32).rearrange("p j (g k u) -> p j g u k", g=PASSES, u=PAIRS)
-            w_grouped[s] = slab_pool.tile([P, PASSES, N_COLS, PACK], BF16, name="w_grouped", align_bytes=64)
-            grouped_words = w_grouped[s][:].bitcast(F32)
+            w_flipped[s] = []
             for g in range(PASSES):
                 bank = psum.tile([P, PAIRS, ROW_TILES, P], F32, tag="bank", name="w_flipped")
                 for u in range(PAIRS):
                     for j in range(ROW_TILES):
-                        nc.tensor.transpose(
-                            out=bank[:, u, j, :],
-                            in_=words[:, j, g, u, :],
-                            identity=ident[:],
-                        )
+                        nc.tensor.transpose(out=bank[:, u, j, :], in_=words[:, j, g, u, :], identity=ident[:])
+                w_flipped[s].append(bank)
+
+        def group_weights(s):
+            w_grouped[s] = slab_pool.tile([P, PASSES, N_COLS, PACK], BF16, name="w_grouped", align_bytes=64)
+            grouped_words = w_grouped[s][:].bitcast(F32)
+            for g in range(PASSES):
                 nc.scalar.copy(
                     out=grouped_words[:, g, :, :].rearrange("p (m j) u -> p m j u", j=ROW_TILES),
-                    in_=bank[:].rearrange("p u j m -> p m j u"),
+                    in_=w_flipped[s][g][:].rearrange("p u j m -> p m j u"),
                 )
 
         def quantise_weights(s):
@@ -244,76 +274,142 @@ def tile_swintransformerblock_pa_kernel(
                 in_=w_grouped[s][:].rearrange("p g c t -> p (g c t)"),
             )
 
-        def project(s):
-            stage = stage_pool.tile([P, HEADS, WS, HD], F32)
-            bias = (
-                bias_all[:, N_COLS * s : N_COLS * (s + 1)]
-                .rearrange("p (a d) -> p a d", d=HD)
-                .unsqueeze(2)
-                .to_broadcast([P, HEADS, PAIR, HD])
-            )
-            for q in range(N_PAIRS):
-                acc = psum.tile([P, PAIR, N_COLS], F32, tag="bank")
-                for i in range(PAIR):
-                    tokens = slice(P * i, P * (i + 1))
-                    for g in range(PASSES):
-                        nc.tensor.matmul_mx(
-                            out=acc[:, i, :],
-                            lhsT=x_codes[:, q, g, tokens].bitcast(FP8X4),
-                            lhsT_scale=x_scales[:, q, g, tokens],
-                            rhs=w_codes[s][:, g, :].bitcast(FP8X4),
-                            rhs_scale=w_scales[s][:, g, :],
-                            start=(g == 0),
-                            stop=(g == PASSES - 1),
-                        )
-                nc.vector.tensor_tensor(
-                    out=stage[:, :, PAIR * q : PAIR * (q + 1), :],
-                    in0=acc[:].rearrange("p i (a d) -> p a i d", d=HD),
-                    in1=bias,
-                    op=ALU.add,
-                )
+        def project(s, width, midway=()):
+            per_bank = BANK_F32 // width
+            heads = width // HD
             slabs_per_output = C // N_COLS
             rows_of = outs[s // slabs_per_output].rearrange("w a (r c) d -> a w r (c d)", c=WS)
-            first_head = HEADS * (s % slabs_per_output)
-            for a in range(HEADS):
-                nc.sync.dma_start(
-                    out=rows_of[first_head + a], in_=stage[:, a, :, :].rearrange("p c d -> p (c d)")
+            for first in range(0, N_COLS, width):
+                stage = stage_pool.tile([P, heads, WS, HD], F32, tag="stage")
+                bias = (
+                    bias_all[:, N_COLS * s + first : N_COLS * s + first + width]
+                    .rearrange("p (a d) -> p a d", d=HD)
+                    .unsqueeze(2)
+                    .to_broadcast([P, heads, per_bank, HD])
                 )
+                for c in range(0, WS, per_bank):
+                    acc = psum.tile([P, per_bank, width], F32, tag="bank")
+                    for i in range(per_bank):
+                        q, j = divmod(c + i, PAIR)
+                        tokens = slice(P * j, P * (j + 1))
+                        for g in range(PASSES):
+                            nc.tensor.matmul_mx(
+                                out=acc[:, i, :],
+                                lhsT=x_codes[:, q, g, tokens].bitcast(FP8X4),
+                                lhsT_scale=x_scales[:, q, g, tokens],
+                                rhs=w_codes[s][:, g, first : first + width].bitcast(FP8X4),
+                                rhs_scale=w_scales[s][:, g, first : first + width],
+                                start=(g == 0),
+                                stop=(g == PASSES - 1),
+                            )
+                    nc.vector.tensor_tensor(
+                        out=stage[:, :, c : c + per_bank, :],
+                        in0=acc[:].rearrange("p i (a d) -> p a i d", d=HD),
+                        in1=bias,
+                        op=ALU.add,
+                    )
+                    if c == 0 and first + width == N_COLS:
+                        for step, slab in midway:
+                            step(slab)
+                first_head = (N_COLS * (s % slabs_per_output) + first) // HD
+                for a in range(heads):
+                    nc.sync.dma_start(
+                        out=rows_of[first_head + a], in_=stage[:, a, :, :].rearrange("p c d -> p (c d)")
+                    )
 
-        for step in range(WS + SCALE_LAG):
-            if step < WS:
-                statistics(step)
-            if 1 <= step <= WS:
-                centre(step - 1)
-            if 1 <= step < FLIP_LAG:
-                flip_weights(step - 1)
-            if step == FLIP_LAG:
-                spread_bias(0)
-                nc.vector.tensor_copy(out=gain[:], in_=gain_bf[:].rearrange("p g t -> p (g t)"))
-                nc.vector.tensor_copy(out=beta[:], in_=beta_bf[:].rearrange("p g t -> p (g t)"))
-            if 0 <= step - FLIP_LAG < WS:
-                flip_tokens(*divmod(step - FLIP_LAG, PASSES))
-            if 0 <= step - SCALE_LAG < WS:
-                scale_tokens(*divmod(step - SCALE_LAG, PASSES))
-        spread_bias(1)
-        spread_bias(2)
+        scalar_sum(1)
+        sums_of(0, 0)
+        sums_of(0, 1)
+        statistics(0)
+        scalar_variance(1)
+        spread_bias(0)
+        flip_weights(0)
+        sums_of(2, 0)
+        invert(0)
+        centre(nc.gpsimd, 0)
+        sums_of(2, 1)
+        sums_of(3, 0)
+        statistics(2)
+        invert(1)
+        centre(nc.gpsimd, 1)
+        sums_of(3, 1)
+        invert(2)
+        centre(nc.gpsimd, 2)
+        sums_of(4, 0)
+        statistics(3)
+        group_weights(0)
+        sums_of(4, 1)
+        invert(3)
+        centre(nc.gpsimd, 3)
+        flip_tokens(0, 0)
+        flip_tokens(0, 1)
+        nc.vector.tensor_copy(out=gain[:], in_=gain_bf[:].rearrange("p g t -> p (g t)"))
+        nc.vector.tensor_copy(out=beta[:], in_=beta_bf[:].rearrange("p g t -> p (g t)"))
+        sums_of(5, 0)
+        statistics(4)
+        scale_tokens(0, 0)
+        sums_of(5, 1)
+        invert(4)
+        centre(nc.gpsimd, 4)
+        sums_of(6, 0)
+        statistics(5)
+        scale_tokens(0, 1)
+        flip_tokens(1, 0)
+        flip_tokens(1, 1)
+        sums_of(6, 1)
+        invert(5)
+        sums_of(7, 0)
+        statistics(6)
+        scale_tokens(1, 0)
+        sums_of(7, 1)
+        invert(6)
+        statistics(7)
+        scale_tokens(1, 1)
+        regroup_tokens(0, 0)
+        centre(nc.vector, 5)
+        flip_tokens(2, 0)
+        flip_tokens(2, 1)
+        scale_tokens(2, 0)
+        scale_tokens(2, 1)
+        invert(7)
+        centre(nc.vector, 6)
+        centre(nc.vector, 7)
+        flip_tokens(3, 0)
+        flip_tokens(3, 1)
+        scale_tokens(3, 0)
+        scale_tokens(3, 1)
+        regroup_tokens(3, 1, nc.scalar.copy)
+        flip_weights(1)
+        group_weights(1)
+        flip_weights(2)
+        group_weights(2)
+        flip_weights(3)
+        group_weights(3)
+        regroup_tokens(0, 1)
+        quantise_tokens(0, 0)
+        regroup_tokens(1, 0)
+        quantise_tokens(0, 1)
+        regroup_tokens(1, 1)
+        quantise_tokens(1, 0)
+        regroup_tokens(2, 0)
+        quantise_tokens(1, 1)
         quantise_weights(0)
-        for unit in range(WS + 1):
-            if unit < WS:
-                regroup_tokens(*divmod(unit, PASSES))
-            if unit > 0:
-                quantise_tokens(*divmod(unit - 1, PASSES))
+        regroup_tokens(2, 1)
+        quantise_tokens(2, 0)
+        regroup_tokens(3, 0)
+        quantise_tokens(2, 1)
+        quantise_tokens(3, 0)
+        quantise_tokens(3, 1)
 
-        sort_weights(2)
-        sort_weights(3)
-        for s in range(0, N_SLABS, 2):
-            project(s)
-            quantise_weights(s + 1)
-            if s + 2 < N_SLABS:
-                flip_weights(s + 2)
-                flip_weights(s + 3)
-                quantise_weights(s + 2)
-            if s + 4 < N_SLABS:
-                sort_weights(s + 4)
-                sort_weights(s + 5)
-            project(s + 1)
+        for s in range(N_SLABS):
+            midway = [(quantise_weights, s + 1)] if s + 1 < N_SLABS else []
+            project(s, N_COLS // 2 if s in (0, N_SLABS - 1) else N_COLS, midway)
+            if s >= 2 and s + 3 + 1 - 2 < N_SLABS:
+                flip_weights(s + 3 + 1 - 2)
+                group_weights(s + 3 + 1 - 2)
+            if 4 <= s + 3 < N_SLABS:
+                sort_weights(s + 3)
+            if s == 1:
+                spread_bias(1)
+            if s == 2:
+                spread_bias(2)

@@ -52,11 +52,14 @@ def tile_swintransformerblock_pa_kernel(
         x_raw = const.tile([P, WS, C], BF16)
         x_rows = x.rearrange("b (q e) k -> (b q) e k", e=WS)
         w_raw = [const.tile([P, ROW_TILES, C], BF16, name="w_raw%d" % s) for s in range(N_SLABS)]
-        bias_row = const.tile([P, 3 * C], BF16)
+        bias_rows = [const.tile([P, C], BF16, name="bias_row%d" % part) for part in range(3)]
         warm = const.tile([P, 2], F32)
         nc.vector.memset(warm[:, 0:1], 1.0)
         nc.scalar.activation(out=warm[:, 1:2], in_=warm[:, 0:1], func=ACT.Sqrt)
-        nc.vector.memset(bias_row[:].bitcast(F32), 0.0)
+        ones = const.tile([P, P], BF16)
+        nc.vector.memset(ones[:], 1.0)
+        for part in range(3):
+            nc.vector.memset(bias_rows[part][:].bitcast(F32), 0.0)
         bias_all = const.tile([P, 3 * C], BF16)
 
         def tile_of(c):
@@ -72,11 +75,12 @@ def tile_swintransformerblock_pa_kernel(
         for half in range(2):
             channels = slice((C // 2) * half, (C // 2) * (half + 1))
             nc.sync.dma_start(out=x_raw[:, SHIFT, channels], in_=x_rows[:, SHIFT, channels])
-        load_tokens(SHIFT + 1, SHIFT + 2)
-        load_tokens(SHIFT + 2, SHIFT + 4)
+        for tile in range(SHIFT + 1, SHIFT + 4):
+            load_tokens(tile, tile + 1)
         load_weights(0)
         load_tokens(SHIFT + 4, WS)
-        load_tokens(0, SHIFT)
+        load_tokens(0, 1)
+        load_tokens(1, SHIFT)
         for s in range(1, N_SLABS):
             load_weights(s)
 
@@ -85,15 +89,18 @@ def tile_swintransformerblock_pa_kernel(
         with nc.allow_non_contiguous_dma(reason="two small vectors, four channels a piece"):
             nc.scalar.dma_start(out=gain_bf[:], in_=norm1_w.rearrange("(g p t) -> p g t", p=P, t=PACK))
             nc.scalar.dma_start(out=beta_bf[:], in_=norm1_b.rearrange("(g p t) -> p g t", p=P, t=PACK))
-        nc.scalar.dma_start(out=bias_row[0:1, :], in_=qkv_b.rearrange("(o n) -> o n", o=1))
         gain = const.tile([P, PLANES], F32)
         beta = const.tile([P, PLANES], F32)
 
-        ones = const.tile([P, P], BF16)
-        nc.vector.memset(ones[:], 1.0)
 
         ident = const.tile([P, P], F32)
         make_identity(nc, ident[:])
+        for part in range(3):
+            queue = nc.gpsimd if part == 0 else nc.scalar
+            queue.dma_start(
+                out=bias_rows[part][0:1, :],
+                in_=qkv_b[C * part : C * (part + 1)].rearrange("(o n) -> o n", o=1),
+            )
         by_grid = ident[:].rearrange("p (b i h) -> p b h i", b=IMAGES, h=2)
         roll_same = const.tile([P, P], F32)
         same = roll_same[:].rearrange("p (b wi wj r) -> p b wi wj r", b=IMAGES, wi=2, wj=2)
@@ -123,6 +130,7 @@ def tile_swintransformerblock_pa_kernel(
         neg_mean = const.tile([P, WS], F32)
         rstd = const.tile([P, WS], F32)
         planes = [const.tile([P, PLANES, PAIR * P], BF16, name="planes%d" % q) for q in range(N_PAIRS)]
+        spread = {}
         stats = {}
         centred = {}
         flipped = {}
@@ -227,16 +235,18 @@ def tile_swintransformerblock_pa_kernel(
 
         def spread_bias(part):
             half = C // 2
-            spread = psum.tile([P, C], BF16, tag="bank")
+            spread[part] = psum.tile([P, C], BF16, tag="bank", name="spread")
             for h in range(2):
                 nc.tensor.matmul(
-                    out=spread[:, half * h : half * (h + 1)],
+                    out=spread[part][:, half * h : half * (h + 1)],
                     lhsT=ones[:],
-                    rhs=bias_row[:, C * part + half * h : C * part + half * (h + 1)],
+                    rhs=bias_rows[part][:, half * h : half * (h + 1)],
                     start=True,
                     stop=True,
                 )
-            nc.scalar.copy(out=bias_all[:, C * part : C * (part + 1)], in_=spread[:])
+
+        def keep_bias(part):
+            nc.scalar.copy(out=bias_all[:, C * part : C * (part + 1)], in_=spread[part][:])
 
         def sort_weights(s):
             w_sorted[s] = sorted_pool.tile([P, ROW_TILES, PASSES, PAIRS, P], F32, name="w_sorted")
@@ -308,7 +318,7 @@ def tile_swintransformerblock_pa_kernel(
                         in1=bias,
                         op=ALU.add,
                     )
-                    if c == 0 and first + width == N_COLS:
+                    if c == 0 and width == N_COLS or c + per_bank == WS and first == 0 and width < N_COLS:
                         for step, slab in midway:
                             step(slab)
                 first_head = (N_COLS * (s % slabs_per_output) + first) // HD
@@ -317,56 +327,57 @@ def tile_swintransformerblock_pa_kernel(
                         out=rows_of[first_head + a], in_=stage[:, a, :, :].rearrange("p c d -> p (c d)")
                     )
 
-        scalar_sum(1)
         sums_of(0, 0)
         sums_of(0, 1)
         statistics(0)
-        scalar_variance(1)
-        spread_bias(0)
-        flip_weights(0)
-        sums_of(2, 0)
+        scalar_sum(2)
+        sums_of(1, 0)
         invert(0)
         centre(nc.gpsimd, 0)
-        sums_of(2, 1)
+        sums_of(1, 1)
         sums_of(3, 0)
-        statistics(2)
+        statistics(1)
+        scalar_variance(2)
+        sums_of(3, 1)
+        spread_bias(0)
+        flip_weights(0)
+        sums_of(4, 0)
         invert(1)
         centre(nc.gpsimd, 1)
-        sums_of(3, 1)
+        statistics(3)
+        sums_of(4, 1)
         invert(2)
         centre(nc.gpsimd, 2)
-        sums_of(4, 0)
-        statistics(3)
-        group_weights(0)
-        sums_of(4, 1)
-        invert(3)
-        centre(nc.gpsimd, 3)
         flip_tokens(0, 0)
         flip_tokens(0, 1)
-        nc.vector.tensor_copy(out=gain[:], in_=gain_bf[:].rearrange("p g t -> p (g t)"))
-        nc.vector.tensor_copy(out=beta[:], in_=beta_bf[:].rearrange("p g t -> p (g t)"))
         sums_of(5, 0)
         statistics(4)
-        scale_tokens(0, 0)
+        group_weights(0)
+        invert(3)
+        centre(nc.gpsimd, 3)
         sums_of(5, 1)
-        invert(4)
-        centre(nc.gpsimd, 4)
         sums_of(6, 0)
         statistics(5)
+        keep_bias(0)
+        nc.vector.tensor_copy(out=gain[:], in_=gain_bf[:].rearrange("p g t -> p (g t)"))
+        nc.vector.tensor_copy(out=beta[:], in_=beta_bf[:].rearrange("p g t -> p (g t)"))
+        scale_tokens(0, 0)
+        sums_of(6, 1)
+        invert(4)
+        sums_of(7, 0)
+        statistics(6)
         scale_tokens(0, 1)
         flip_tokens(1, 0)
         flip_tokens(1, 1)
-        sums_of(6, 1)
         invert(5)
-        sums_of(7, 0)
-        statistics(6)
-        scale_tokens(1, 0)
         sums_of(7, 1)
-        invert(6)
         statistics(7)
+        scale_tokens(1, 0)
         scale_tokens(1, 1)
-        regroup_tokens(0, 0)
+        centre(nc.vector, 4)
         centre(nc.vector, 5)
+        regroup_tokens(0, 0)
+        invert(6)
         flip_tokens(2, 0)
         flip_tokens(2, 1)
         scale_tokens(2, 0)
@@ -411,5 +422,7 @@ def tile_swintransformerblock_pa_kernel(
                 sort_weights(s + 3)
             if s == 1:
                 spread_bias(1)
+                keep_bias(1)
             if s == 2:
                 spread_bias(2)
+                keep_bias(2)

@@ -323,7 +323,8 @@ def tile_swintransformerblock_pa_kernel(
                             step(slab)
                 first_head = (N_COLS * (s % slabs_per_output) + first) // HD
                 for a in range(heads):
-                    nc.sync.dma_start(
+                    queue = nc.gpsimd if a % 4 == 3 and s < N_SLABS - 1 else nc.sync
+                    queue.dma_start(
                         out=rows_of[first_head + a], in_=stage[:, a, :, :].rearrange("p c d -> p (c d)")
                     )
 

@@ -43,10 +43,10 @@ def tile_swintransformerblock_pa_kernel(
         const = ctx.enter_context(tc.tile_pool(name="const", bufs=1))
         small = ctx.enter_context(tc.tile_pool(name="small", bufs=4))
         centred_pool = ctx.enter_context(tc.tile_pool(name="centred", bufs=3))
-        work = ctx.enter_context(tc.tile_pool(name="work", bufs=4))
+        work = ctx.enter_context(tc.tile_pool(name="work", bufs=3))
         slab_pool = ctx.enter_context(tc.tile_pool(name="slab", bufs=4))
-        sorted_pool = ctx.enter_context(tc.tile_pool(name="sorted", bufs=3))
-        stage_pool = ctx.enter_context(tc.tile_pool(name="stage", bufs=4))
+        sorted_pool = ctx.enter_context(tc.tile_pool(name="sorted", bufs=2))
+        stage_pool = ctx.enter_context(tc.tile_pool(name="stage", bufs=5))
         psum = ctx.enter_context(tc.psum_pool(name="psum", bufs=BANKS))
 
         x_raw = const.tile([P, WS, C], BF16)
@@ -77,8 +77,8 @@ def tile_swintransformerblock_pa_kernel(
             nc.sync.dma_start(out=x_raw[:, SHIFT, channels], in_=x_rows[:, SHIFT, channels])
         for tile in range(SHIFT + 1, SHIFT + 4):
             load_tokens(tile, tile + 1)
-        load_weights(0)
         load_tokens(SHIFT + 4, WS)
+        load_weights(0)
         load_tokens(0, 1)
         load_tokens(1, SHIFT)
         for s in range(1, N_SLABS):
@@ -176,8 +176,8 @@ def tile_swintransformerblock_pa_kernel(
                 out=std[:, c : c + 1], in_=sums[:, c, 1:2], func=ACT.Sqrt, bias=EPS, scale=1.0 / C
             )
 
-        def invert(c):
-            nc.vector.reciprocal(out=rstd[:, c : c + 1], in_=std[:, c : c + 1])
+        def invert(first, last):
+            nc.vector.reciprocal(out=rstd[:, first : last + 1], in_=std[:, first : last + 1])
 
         def centre(engine, c):
             q, i = divmod(c, PAIR)
@@ -226,27 +226,29 @@ def tile_swintransformerblock_pa_kernel(
                 in_=planes[q][:, PACK * g : PACK * (g + 1), :].rearrange("p t (m i) -> p m t i", i=4),
             )
 
-        def quantise_tokens(q, g):
+        def quantise_tokens(q, first, last):
+            units = slice(first, last + 1)
             nc.vector.quantize_mx(
-                out=x_codes[:, q, g, :].bitcast(FP8X4),
-                scales=x_scales[:, q, g, :],
-                in_=grouped[q][:, g, :, :].rearrange("p m t -> p (m t)"),
+                out=x_codes[:, q, units, :].rearrange("p g m -> p (g m)").bitcast(FP8X4),
+                scales=x_scales[:, q, units, :].rearrange("p g m -> p (g m)"),
+                in_=grouped[q][:, units, :, :].rearrange("p g m t -> p (g m t)"),
             )
 
-        def spread_bias(part):
-            half = C // 2
-            spread[part] = psum.tile([P, C], BF16, tag="bank", name="spread")
-            for h in range(2):
+        def spread_bias(first, last):
+            spread[first] = psum.tile([P, last - first], BF16, tag="bank", name="spread")
+            part, start = divmod(first, C)
+            for column in range(0, last - first, BANK_F32):
+                width = min(BANK_F32, last - first - column)
                 nc.tensor.matmul(
-                    out=spread[part][:, half * h : half * (h + 1)],
+                    out=spread[first][:, column : column + width],
                     lhsT=ones[:],
-                    rhs=bias_rows[part][:, half * h : half * (h + 1)],
+                    rhs=bias_rows[part][:, start + column : start + column + width],
                     start=True,
                     stop=True,
                 )
 
-        def keep_bias(part):
-            nc.scalar.copy(out=bias_all[:, C * part : C * (part + 1)], in_=spread[part][:])
+        def keep_bias(first, last):
+            nc.scalar.copy(out=bias_all[:, first:last], in_=spread[first][:])
 
         def sort_weights(s):
             w_sorted[s] = sorted_pool.tile([P, ROW_TILES, PASSES, PAIRS, P], F32, name="w_sorted")
@@ -333,44 +335,44 @@ def tile_swintransformerblock_pa_kernel(
         statistics(0)
         scalar_sum(2)
         sums_of(1, 0)
-        invert(0)
+        invert(0, 0)
         centre(nc.gpsimd, 0)
+        nc.gpsimd.tensor_copy(out=gain[:], in_=gain_bf[:].rearrange("p g t -> p (g t)"))
+        nc.gpsimd.tensor_copy(out=beta[:], in_=beta_bf[:].rearrange("p g t -> p (g t)"))
         sums_of(1, 1)
         sums_of(3, 0)
         statistics(1)
         scalar_variance(2)
         sums_of(3, 1)
-        spread_bias(0)
+        spread_bias(0, N_COLS)
         flip_weights(0)
-        sums_of(4, 0)
-        invert(1)
+        invert(1, 1)
         centre(nc.gpsimd, 1)
+        sums_of(4, 0)
         statistics(3)
         sums_of(4, 1)
-        invert(2)
+        invert(2, 2)
         centre(nc.gpsimd, 2)
         flip_tokens(0, 0)
         flip_tokens(0, 1)
         sums_of(5, 0)
         statistics(4)
         group_weights(0)
-        invert(3)
+        invert(3, 3)
         centre(nc.gpsimd, 3)
         sums_of(5, 1)
         sums_of(6, 0)
         statistics(5)
-        keep_bias(0)
-        nc.vector.tensor_copy(out=gain[:], in_=gain_bf[:].rearrange("p g t -> p (g t)"))
-        nc.vector.tensor_copy(out=beta[:], in_=beta_bf[:].rearrange("p g t -> p (g t)"))
+        keep_bias(0, N_COLS)
         scale_tokens(0, 0)
         sums_of(6, 1)
-        invert(4)
+        invert(4, 4)
         sums_of(7, 0)
         statistics(6)
         scale_tokens(0, 1)
         flip_tokens(1, 0)
         flip_tokens(1, 1)
-        invert(5)
+        invert(5, 5)
         sums_of(7, 1)
         statistics(7)
         scale_tokens(1, 0)
@@ -378,12 +380,11 @@ def tile_swintransformerblock_pa_kernel(
         centre(nc.vector, 4)
         centre(nc.vector, 5)
         regroup_tokens(0, 0)
-        invert(6)
         flip_tokens(2, 0)
         flip_tokens(2, 1)
         scale_tokens(2, 0)
         scale_tokens(2, 1)
-        invert(7)
+        invert(6, 7)
         centre(nc.vector, 6)
         centre(nc.vector, 7)
         flip_tokens(3, 0)
@@ -395,23 +396,22 @@ def tile_swintransformerblock_pa_kernel(
         group_weights(1)
         flip_weights(2)
         group_weights(2)
+        spread_bias(N_COLS, C)
+        keep_bias(N_COLS, C)
         flip_weights(3)
         group_weights(3)
-        regroup_tokens(0, 1)
-        quantise_tokens(0, 0)
-        regroup_tokens(1, 0)
-        quantise_tokens(0, 1)
-        regroup_tokens(1, 1)
-        quantise_tokens(1, 0)
-        regroup_tokens(2, 0)
-        quantise_tokens(1, 1)
-        quantise_weights(0)
-        regroup_tokens(2, 1)
-        quantise_tokens(2, 0)
-        regroup_tokens(3, 0)
-        quantise_tokens(2, 1)
-        quantise_tokens(3, 0)
-        quantise_tokens(3, 1)
+        for q in range(N_PAIRS - 1):
+            for g in range(PASSES):
+                if (q, g) != (0, 0):
+                    regroup_tokens(q, g)
+            if q > 0:
+                quantise_tokens(q - 1, 0, PASSES - 1)
+            if q == N_PAIRS // 2:
+                quantise_weights(0)
+        regroup_tokens(N_PAIRS - 1, 0)
+        quantise_tokens(N_PAIRS - 2, 0, PASSES - 1)
+        quantise_tokens(N_PAIRS - 1, 0, 0)
+        quantise_tokens(N_PAIRS - 1, 1, 1)
 
         for s in range(N_SLABS):
             midway = [(quantise_weights, s + 1)] if s + 1 < N_SLABS else []
@@ -422,8 +422,8 @@ def tile_swintransformerblock_pa_kernel(
             if 4 <= s + 3 < N_SLABS:
                 sort_weights(s + 3)
             if s == 1:
-                spread_bias(1)
-                keep_bias(1)
+                spread_bias(C, 2 * C)
+                keep_bias(C, 2 * C)
             if s == 2:
-                spread_bias(2)
-                keep_bias(2)
+                spread_bias(2 * C, 3 * C)
+                keep_bias(2 * C, 3 * C)

from contextlib import ExitStack

import concourse.mybir as mybir
from concourse.masks import make_identity

F32 = mybir.dt.float32
BF16 = mybir.dt.bfloat16
U32 = mybir.dt.uint32
U8 = mybir.dt.uint8
FP8X4 = mybir.dt.float8_e4m3fn_x4
ALU = mybir.AluOpType
ACT = mybir.ActivationFunctionType

P = 128
C = 1024
EPS = 1e-5
IMAGES, GRID, WS, SHIFT = 4, 16, 8, 3
HD = 32
PACK = 4
PASSES = C // (P * PACK)
PLANES = C // P
PAIRS = PACK // 2
PAIR = 2
N_PAIRS = WS // PAIR
N_COLS = 256
N_SLABS = 3 * C // N_COLS
ROW_TILES = N_COLS // P
HEADS = N_COLS // HD
BANKS = 8
BANK_F32 = 512

FLOPS = 2 * IMAGES * GRID * GRID * C * 3 * C


def tile_swintransformerblock_pa_kernel(
    tc, x, norm1_w, norm1_b, qkv_w, qkv_b, out_0, out_1, out_2
):
    nc = tc.nc
    outs = (out_0, out_1, out_2)

    with ExitStack() as ctx:
        ctx.enter_context(tc.manual_schedule())
        const = ctx.enter_context(tc.tile_pool(name="const", bufs=1))
        small = ctx.enter_context(tc.tile_pool(name="small", bufs=4))
        centred_pool = ctx.enter_context(tc.tile_pool(name="centred", bufs=3))
        work = ctx.enter_context(tc.tile_pool(name="work", bufs=3))
        slab_pool = ctx.enter_context(tc.tile_pool(name="slab", bufs=4))
        sorted_pool = ctx.enter_context(tc.tile_pool(name="sorted", bufs=2))
        stage_pool = ctx.enter_context(tc.tile_pool(name="stage", bufs=5))
        psum = ctx.enter_context(tc.psum_pool(name="psum", bufs=BANKS))

        x_raw = const.tile([P, WS, C], BF16)
        x_rows = x.rearrange("b (q e) k -> (b q) e k", e=WS)
        w_raw = [const.tile([P, ROW_TILES, C], BF16, name="w_raw%d" % s) for s in range(N_SLABS)]
        bias_rows = [const.tile([P, C], BF16, name="bias_row%d" % part) for part in range(3)]
        warm = const.tile([P, 2], F32)
        nc.vector.memset(warm[:, 0:1], 1.0)
        nc.scalar.activation(out=warm[:, 1:2], in_=warm[:, 0:1], func=ACT.Sqrt)
        ones = const.tile([P, P], BF16)
        nc.vector.memset(ones[:], 1.0)
        for part in range(3):
            nc.vector.memset(bias_rows[part][:].bitcast(F32), 0.0)
        bias_all = const.tile([P, 3 * C], BF16)

        def tile_of(c):
            return (c + SHIFT) % WS

        def load_tokens(first, last):
            nc.sync.dma_start(out=x_raw[:, first:last, :], in_=x_rows[:, first:last, :])

        def load_weights(s):
            rows = qkv_w[N_COLS * s : N_COLS * (s + 1), :]
            nc.sync.dma_start(out=w_raw[s][:], in_=rows.rearrange("(p j) k -> p j k", p=P))

        for half in range(2):
            channels = slice((C // 2) * half, (C // 2) * (half + 1))
            nc.sync.dma_start(out=x_raw[:, SHIFT, channels], in_=x_rows[:, SHIFT, channels])
        for tile in range(SHIFT + 1, SHIFT + 4):
            load_tokens(tile, tile + 1)
        load_tokens(SHIFT + 4, WS)
        load_weights(0)
        load_tokens(0, 1)
        load_tokens(1, SHIFT)
        for s in range(1, N_SLABS):
            load_weights(s)

        gain_bf = const.tile([P, PASSES, PACK], BF16)
        beta_bf = const.tile([P, PASSES, PACK], BF16)
        with nc.allow_non_contiguous_dma(reason="two small vectors, four channels a piece"):
            nc.scalar.dma_start(out=gain_bf[:], in_=norm1_w.rearrange("(g p t) -> p g t", p=P, t=PACK))
            nc.scalar.dma_start(out=beta_bf[:], in_=norm1_b.rearrange("(g p t) -> p g t", p=P, t=PACK))
        gain = const.tile([P, PLANES], F32)
        beta = const.tile([P, PLANES], F32)


        ident = const.tile([P, P], F32)
        make_identity(nc, ident[:])
        for part in range(3):
            queue = nc.gpsimd if part == 0 else nc.scalar
            queue.dma_start(
                out=bias_rows[part][0:1, :],
                in_=qkv_b[C * part : C * (part + 1)].rearrange("(o n) -> o n", o=1),
            )
        by_grid = ident[:].rearrange("p (b i h) -> p b h i", b=IMAGES, h=2)
        roll_same = const.tile([P, P], F32)
        same = roll_same[:].rearrange("p (b wi wj r) -> p b wi wj r", b=IMAGES, wi=2, wj=2)
        wrap = GRID - WS - SHIFT
        nc.vector.tensor_copy(out=same[:, :, 0, :, :], in_=by_grid[:, :, :, SHIFT : SHIFT + WS])
        nc.vector.tensor_copy(out=same[:, :, 1, :, 0:wrap], in_=by_grid[:, :, :, SHIFT + WS : GRID])
        nc.vector.tensor_copy(out=same[:, :, 1, :, wrap:WS], in_=by_grid[:, :, :, 0:SHIFT])
        roll_swap = const.tile([P, P], F32)
        swap = roll_swap[:].rearrange("p (b wi wj r) -> p b wi wj r", b=IMAGES, wi=2, wj=2)
        nc.vector.tensor_copy(out=swap[:, :, :, 0, :], in_=same[:, :, :, 1, :])
        nc.vector.tensor_copy(out=swap[:, :, :, 1, :], in_=same[:, :, :, 0, :])

        x_codes = const.tile([P, N_PAIRS, PASSES, PAIR * P], U32, align_bytes=64)
        x_scales = const.tile([P, N_PAIRS, PASSES, PAIR * P], U8, align_bytes=64)
        w_codes = [
            const.tile([P, PASSES, N_COLS], U32, name="w_codes%d" % s, align_bytes=64)
            for s in range(N_SLABS)
        ]
        w_scales = [
            const.tile([P, PASSES, N_COLS], U8, name="w_scales%d" % s, align_bytes=64)
            for s in range(N_SLABS)
        ]
        mean_var = const.tile([P, WS, 2], F32)
        std = const.tile([P, WS], F32)
        sums = const.tile([P, WS, 2], F32)
        ignored = const.tile([P, C], BF16)
        neg_mean = const.tile([P, WS], F32)
        rstd = const.tile([P, WS], F32)
        planes = [const.tile([P, PLANES, PAIR * P], BF16, name="planes%d" % q) for q in range(N_PAIRS)]
        spread = {}
        stats = {}
        centred = {}
        flipped = {}
        grouped = {}
        w_sorted = {}
        w_flipped = {}
        w_grouped = {}

        def sums_of(c, half):
            if half == 0:
                stats[c] = small.tile([P, 2, 6], F32, name="stats")
            nc.vector.bn_stats(
                out=stats[c][:, half, :],
                in_=x_raw[:, tile_of(c), (C // 2) * half : (C // 2) * (half + 1)],
            )

        def statistics(c):
            nc.vector.bn_aggr(out=mean_var[:, c, :], in_=stats[c][:].rearrange("p h s -> p (h s)"))
            nc.scalar.activation(
                out=std[:, c : c + 1], in_=mean_var[:, c, 1:2], func=ACT.Sqrt, bias=EPS, scale=1.0
            )
            nc.scalar.activation(
                out=neg_mean[:, c : c + 1], in_=mean_var[:, c, 0:1], func=ACT.Identity, scale=-1.0
            )

        def scalar_sum(c):
            nc.scalar.activation(
                out=ignored[:], in_=x_raw[:, tile_of(c), :], func=ACT.Identity, accum_out=sums[:, c, 0:1]
            )
            nc.scalar.activation(
                out=neg_mean[:, c : c + 1], in_=sums[:, c, 0:1], func=ACT.Identity, scale=-1.0 / C
            )

        def scalar_variance(c):
            nc.scalar.activation(
                out=ignored[:],
                in_=x_raw[:, tile_of(c), :],
                func=ACT.Square,
                bias=neg_mean[:, c : c + 1],
                accum_out=sums[:, c, 1:2],
            )
            nc.scalar.activation(
                out=std[:, c : c + 1], in_=sums[:, c, 1:2], func=ACT.Sqrt, bias=EPS, scale=1.0 / C
            )

        def invert(first, last):
            nc.vector.reciprocal(out=rstd[:, first : last + 1], in_=std[:, first : last + 1])

        def centre(engine, c):
            q, i = divmod(c, PAIR)
            if i == 0:
                centred[q] = centred_pool.tile([P, PAIR, C], F32, name="centred")
            engine.tensor_scalar(
                out=centred[q][:, i, :].rearrange("p (g t k) -> p g t k", g=PASSES, t=PACK),
                in0=x_raw[:, tile_of(c), :].rearrange("p (g k t) -> p g t k", g=PASSES, t=PACK),
                scalar1=neg_mean[:, c : c + 1],
                scalar2=rstd[:, c : c + 1],
                op0=ALU.add,
                op1=ALU.mult,
            )

        def flip_tokens(q, g):
            flipped[q, g] = []
            for u in range(2):
                bank = psum.tile([P, 2, PAIR, P], F32, tag="bank", name="flipped")
                for e in range(2):
                    plane = PACK * g + 2 * u + e
                    for i in range(PAIR):
                        nc.tensor.transpose(
                            out=bank[:, e, i, :],
                            in_=centred[q][:, i, P * plane : P * (plane + 1)],
                            identity=(roll_same if PAIR * q + i < WS - SHIFT else roll_swap)[:],
                        )
                flipped[q, g].append(bank)

        def scale_tokens(q, g):
            for u in range(2):
                for e in range(2):
                    plane = PACK * g + 2 * u + e
                    nc.scalar.activation(
                        out=planes[q][:, plane, :],
                        in_=flipped[q, g][u][:, e, :, :].rearrange("p i m -> p (i m)"),
                        func=ACT.Identity,
                        scale=gain[:, plane : plane + 1],
                        bias=beta[:, plane : plane + 1],
                    )

        def regroup_tokens(q, g, copy=nc.vector.tensor_copy):
            if q not in grouped:
                grouped[q] = work.tile([P, PASSES, PAIR * P, PACK], BF16, name="grouped", align_bytes=64)
            copy(
                out=grouped[q][:, g, :, :].rearrange("p (m i) t -> p m t i", i=4),
                in_=planes[q][:, PACK * g : PACK * (g + 1), :].rearrange("p t (m i) -> p m t i", i=4),
            )

        def quantise_tokens(q, first, last):
            units = slice(first, last + 1)
            nc.vector.quantize_mx(
                out=x_codes[:, q, units, :].rearrange("p g m -> p (g m)").bitcast(FP8X4),
                scales=x_scales[:, q, units, :].rearrange("p g m -> p (g m)"),
                in_=grouped[q][:, units, :, :].rearrange("p g m t -> p (g m t)"),
            )

        def spread_bias(first, last):
            spread[first] = psum.tile([P, last - first], BF16, tag="bank", name="spread")
            part, start = divmod(first, C)
            for column in range(0, last - first, BANK_F32):
                width = min(BANK_F32, last - first - column)
                nc.tensor.matmul(
                    out=spread[first][:, column : column + width],
                    lhsT=ones[:],
                    rhs=bias_rows[part][:, start + column : start + column + width],
                    start=True,
                    stop=True,
                )

        def keep_bias(first, last):
            nc.scalar.copy(out=bias_all[:, first:last], in_=spread[first][:])

        def sort_weights(s):
            w_sorted[s] = sorted_pool.tile([P, ROW_TILES, PASSES, PAIRS, P], F32, name="w_sorted")
            nc.scalar.copy(
                out=w_sorted[s][:].rearrange("p j g u k -> p (j g) u k"),
                in_=w_raw[s][:].bitcast(F32).rearrange("p j (g k u) -> p (j g) u k", g=PASSES, u=PAIRS),
            )

        def flip_weights(s):
            if s in w_sorted:
                words = w_sorted[s][:]
            else:
                words = w_raw[s][:].bitcast(F32).rearrange("p j (g k u) -> p j g u k", g=PASSES, u=PAIRS)
            w_flipped[s] = []
            for g in range(PASSES):
                bank = psum.tile([P, PAIRS, ROW_TILES, P], F32, tag="bank", name="w_flipped")
                for u in range(PAIRS):
                    for j in range(ROW_TILES):
                        nc.tensor.transpose(out=bank[:, u, j, :], in_=words[:, j, g, u, :], identity=ident[:])
                w_flipped[s].append(bank)

        def group_weights(s):
            w_grouped[s] = slab_pool.tile([P, PASSES, N_COLS, PACK], BF16, name="w_grouped", align_bytes=64)
            grouped_words = w_grouped[s][:].bitcast(F32)
            for g in range(PASSES):
                nc.scalar.copy(
                    out=grouped_words[:, g, :, :].rearrange("p (m j) u -> p m j u", j=ROW_TILES),
                    in_=w_flipped[s][g][:].rearrange("p u j m -> p m j u"),
                )

        def quantise_weights(s):
            nc.vector.quantize_mx(
                out=w_codes[s][:].rearrange("p g c -> p (g c)").bitcast(FP8X4),
                scales=w_scales[s][:].rearrange("p g c -> p (g c)"),
                in_=w_grouped[s][:].rearrange("p g c t -> p (g c t)"),
            )

        def project(s, width, midway=()):
            per_bank = BANK_F32 // width
            heads = width // HD
            slabs_per_output = C // N_COLS
            rows_of = outs[s // slabs_per_output].rearrange("w a (r c) d -> a w r (c d)", c=WS)
            for first in range(0, N_COLS, width):
                stage = stage_pool.tile([P, heads, WS, HD], F32, tag="stage")
                bias = (
                    bias_all[:, N_COLS * s + first : N_COLS * s + first + width]
                    .rearrange("p (a d) -> p a d", d=HD)
                    .unsqueeze(2)
                    .to_broadcast([P, heads, per_bank, HD])
                )
                for c in range(0, WS, per_bank):
                    acc = psum.tile([P, per_bank, width], F32, tag="bank")
                    for i in range(per_bank):
                        q, j = divmod(c + i, PAIR)
                        tokens = slice(P * j, P * (j + 1))
                        for g in range(PASSES):
                            nc.tensor.matmul_mx(
                                out=acc[:, i, :],
                                lhsT=x_codes[:, q, g, tokens].bitcast(FP8X4),
                                lhsT_scale=x_scales[:, q, g, tokens],
                                rhs=w_codes[s][:, g, first : first + width].bitcast(FP8X4),
                                rhs_scale=w_scales[s][:, g, first : first + width],
                                start=(g == 0),
                                stop=(g == PASSES - 1),
                            )
                    nc.vector.tensor_tensor(
                        out=stage[:, :, c : c + per_bank, :],
                        in0=acc[:].rearrange("p i (a d) -> p a i d", d=HD),
                        in1=bias,
                        op=ALU.add,
                    )
                    if c == 0 and width == N_COLS or c + per_bank == WS and first == 0 and width < N_COLS:
                        for step, slab in midway:
                            step(slab)
                first_head = (N_COLS * (s % slabs_per_output) + first) // HD
                for a in range(heads):
                    queue = nc.gpsimd if a % 4 == 3 and s < N_SLABS - 1 else nc.sync
                    queue.dma_start(
                        out=rows_of[first_head + a], in_=stage[:, a, :, :].rearrange("p c d -> p (c d)")
                    )

        sums_of(0, 0)
        sums_of(0, 1)
        statistics(0)
        scalar_sum(2)
        sums_of(1, 0)
        invert(0, 0)
        centre(nc.gpsimd, 0)
        nc.gpsimd.tensor_copy(out=gain[:], in_=gain_bf[:].rearrange("p g t -> p (g t)"))
        nc.gpsimd.tensor_copy(out=beta[:], in_=beta_bf[:].rearrange("p g t -> p (g t)"))
        sums_of(1, 1)
        sums_of(3, 0)
        statistics(1)
        scalar_variance(2)
        sums_of(3, 1)
        spread_bias(0, N_COLS)
        flip_weights(0)
        invert(1, 1)
        centre(nc.gpsimd, 1)
        sums_of(4, 0)
        statistics(3)
        sums_of(4, 1)
        invert(2, 2)
        centre(nc.gpsimd, 2)
        flip_tokens(0, 0)
        flip_tokens(0, 1)
        sums_of(5, 0)
        statistics(4)
        group_weights(0)
        invert(3, 3)
        centre(nc.gpsimd, 3)
        sums_of(5, 1)
        sums_of(6, 0)
        statistics(5)
        keep_bias(0, N_COLS)
        scale_tokens(0, 0)
        sums_of(6, 1)
        invert(4, 4)
        sums_of(7, 0)
        statistics(6)
        scale_tokens(0, 1)
        flip_tokens(1, 0)
        flip_tokens(1, 1)
        invert(5, 5)
        sums_of(7, 1)
        statistics(7)
        scale_tokens(1, 0)
        scale_tokens(1, 1)
        centre(nc.vector, 4)
        centre(nc.vector, 5)
        regroup_tokens(0, 0)
        flip_tokens(2, 0)
        flip_tokens(2, 1)
        scale_tokens(2, 0)
        scale_tokens(2, 1)
        invert(6, 7)
        centre(nc.vector, 6)
        centre(nc.vector, 7)
        flip_tokens(3, 0)
        flip_tokens(3, 1)
        scale_tokens(3, 0)
        scale_tokens(3, 1)
        regroup_tokens(3, 1, nc.scalar.copy)
        flip_weights(1)
        group_weights(1)
        flip_weights(2)
        group_weights(2)
        spread_bias(N_COLS, C)
        keep_bias(N_COLS, C)
        flip_weights(3)
        group_weights(3)
        for q in range(N_PAIRS - 1):
            for g in range(PASSES):
                if (q, g) != (0, 0):
                    regroup_tokens(q, g)
            if q > 0:
                quantise_tokens(q - 1, 0, PASSES - 1)
            if q == N_PAIRS // 2:
                quantise_weights(0)
        regroup_tokens(N_PAIRS - 1, 0)
        quantise_tokens(N_PAIRS - 2, 0, PASSES - 1)
        quantise_tokens(N_PAIRS - 1, 0, 0)
        quantise_tokens(N_PAIRS - 1, 1, 1)

        for s in range(N_SLABS):
            midway = [(quantise_weights, s + 1)] if s + 1 < N_SLABS else []
            project(s, N_COLS // 2 if s in (0, N_SLABS - 1) else N_COLS, midway)
            if s >= 2 and s + 3 + 1 - 2 < N_SLABS:
                flip_weights(s + 3 + 1 - 2)
                group_weights(s + 3 + 1 - 2)
            if 4 <= s + 3 < N_SLABS:
                sort_weights(s + 3)
            if s == 1:
                spread_bias(C, 2 * C)
                keep_bias(C, 2 * C)
            if s == 2:
                spread_bias(2 * C, 3 * C)
                keep_bias(2 * C, 3 * C)
